import numpy as np
import ml_dtypes


def mxq(x, axis, fmt="e4m3"):
    dtype, down = {"e4m3": (ml_dtypes.float8_e4m3fn, 7), "e5m2": (ml_dtypes.float8_e5m2, 14)}[fmt]
    v = np.moveaxis(np.asarray(x, np.float32).astype(ml_dtypes.bfloat16).astype(np.float64), axis, -1)
    blocks = v.reshape(v.shape[:-1] + (-1, 32))
    amax = np.abs(blocks).max(-1, keepdims=True)
    byte = np.maximum(np.where(amax > 0, np.frexp(amax)[1] - 1 + 127, 0) - down, 1)
    scale = np.exp2(byte - 127.0)
    codes = (blocks / scale).astype(np.float32).astype(dtype).astype(np.float64)
    return np.moveaxis((codes * scale).reshape(v.shape), -1, axis)


WIDE = False


def mx_kscale(k):
    if not WIDE:
        return np.ones(k)
    levels = np.array([10, -10, 5, -5, 0])
    if k % 512:
        return np.exp2(np.random.permutation(np.resize(levels, k // 32))).repeat(32)
    a = np.empty((k // 512, 16))
    for p in range(k // 512):
        a[p, :8] = np.random.permutation(np.resize(levels, 8))
        for g in range(8):
            far = levels[np.abs(levels - a[p, g]) >= 10]
            a[p, g + 8] = far[np.random.randint(len(far))]
    return np.exp2(a.ravel()).repeat(32)


BF16 = ml_dtypes.bfloat16


def bf(x):
    return np.asarray(x, np.float32).astype(BF16)


def f64(x):
    return np.asarray(x).astype(np.float64)


B, N, NFEAT, NHID, NHID2, NCLASS = 2, 1024, 512, 512, 1024, 256


def setup_inputs():
    t, s = mx_kscale(NFEAT), mx_kscale(N)
    return {"x": bf(np.random.standard_normal((B, N, NFEAT)) * t / s[:, None]),
            "adj": bf(np.random.uniform(size=(N, N)) * s),
            "S": bf(np.random.standard_normal((N, N)) * 1.7 / np.sqrt(N)),
            "W1": bf(np.random.standard_normal((NFEAT, NHID)) / np.sqrt(NFEAT) / t[:, None])}


def reference(x, adj, S, W1):
    support = f64(bf(mxq(f64(x), 2, "e4m3") @ mxq(f64(W1), 0, "e4m3")))
    weighting = f64(adj) * f64(S)
    out = mxq(weighting, 1, "e4m3") @ mxq(support, 1, "e4m3")
    return np.maximum(out, 0.0)

@@ -1,0 +1,233 @@
+from contextlib import ExitStack
+
+import concourse.mybir as mybir
+from concourse.masks import make_identity
+
+F32 = mybir.dt.float32
+BF16 = mybir.dt.bfloat16
+U32 = mybir.dt.uint32
+U8 = mybir.dt.uint8
+FP8X4 = mybir.dt.float8_e4m3fn_x4
+RELU = mybir.ActivationFunctionType.Relu
+MULT = mybir.AluOpType.mult
+
+B, N, F, H = 2, 1024, 512, 512
+FLOPS = 2 * B * N * F * H + 2 * B * N * N * H
+P = 128
+S1_DT = BF16
+N_HEAT = 6
+
+
+def tile_gcn_pa_kernel(tc, x, adj, S, W1, out):
+    nc = tc.nc
+    with ExitStack() as ctx:
+        keep = ctx.enter_context(tc.tile_pool(name="keep", bufs=1))
+        tp_pool = ctx.enter_context(tc.psum_pool(name="tp", bufs=3))
+        mm_pool = ctx.enter_context(tc.psum_pool(name="mm", bufs=5))
+        ctx.enter_context(tc.manual_schedule())
+
+        ident = keep.tile([P, P], F32, name="ident")
+        make_identity(nc, ident[:])
+        warm = keep.tile([P, 8], F32, name="warm")
+        warm2 = keep.tile([P, 8], F32, name="warm2")
+        nc.vector.memset(warm[:], 0.0)
+        nc.scalar.activation(out=warm2[:], in_=warm[:], func=RELU)
+
+        zeros = keep.tile([P, 512], BF16, name="zeros")
+        nc.vector.memset(zeros[:], 0.0)
+        heat = mm_pool.tile([P, 512], F32, name="heat", tag="mm")
+        for k in range(N_HEAT):
+            nc.tensor.matmul(out=heat[:], lhsT=zeros[:, 0:P], rhs=zeros[:], start=True, stop=True)
+
+        w1r = keep.tile([P, 4, H], BF16, name="w1r")
+        nc.sync.dma_start(out=w1r[:], in_=W1.rearrange("(p j) c -> p j c", j=4))
+        xf = x.rearrange("b m f -> (b m) f")
+        xr, adj_sb, s_sb = [], [], []
+
+        def load_x(q):
+            src = xf[512 * q : 512 * (q + 1), :].rearrange("(m t) f -> m t f", t=4)
+            halves = []
+            for a in range(2):
+                t_ = keep.tile([P, 2, F], BF16, name="xr%d_%d" % (q, a))
+                nc.sync.dma_start(out=t_[:], in_=src[:, 2 * a : 2 * a + 2, :])
+                halves.append(t_)
+            xr.append(halves)
+
+        def load_w(u):
+            a_ = keep.tile([P, 2, N], BF16, name="adj%d" % u)
+            nc.sync.dma_start(out=a_[:], in_=adj[256 * u : 256 * (u + 1), :].rearrange("(i p) m -> p i m", p=P))
+            s_ = keep.tile([P, 2, N], BF16, name="s%d" % u)
+            nc.sync.dma_start(out=s_[:], in_=S[256 * u : 256 * (u + 1), :].rearrange("(i p) m -> p i m", p=P))
+            adj_sb.append(a_)
+            s_sb.append(s_)
+
+        load_x(0)
+        load_x(1)
+        load_x(2)
+        load_w(0)
+        load_x(3)
+        load_w(1)
+        load_w(2)
+        load_w(3)
+
+        def mx_tiles(tag):
+            g = keep.tile([P, 2048], BF16, name=tag + "g", align_bytes=64)
+            c = keep.tile([P, 512], U32, name=tag + "c", align_bytes=64)
+            s = keep.tile([P, 512], U8, name=tag + "s", align_bytes=64)
+            return g, c, s
+
+        def quant(t3):
+            g, c, s = t3
+            nc.vector.quantize_mx(out=c[:].bitcast(FP8X4), scales=s[:], in_=g[:])
+
+        def copy_on(eng, out_, in_):
+            if eng == "S":
+                nc.scalar.copy(out=out_, in_=in_)
+            else:
+                nc.vector.tensor_copy(out=out_, in_=in_)
+
+        w1m = mx_tiles("w1")
+        xm = [mx_tiles("x%d" % q) for q in range(4)]
+        sm = [mx_tiles("sp%d" % q) for q in range(4)]
+        wm = [mx_tiles("w%d" % u) for u in range(4)]
+        wprod = [keep.tile([P, 2, N], BF16, name="wprod%d" % u) for u in range(4)]
+
+        nc.vector.tensor_copy(
+            out=w1m[0][:].rearrange("p (c j) -> p c j", j=4),
+            in_=w1r[:].rearrange("p j c -> p c j"),
+        )
+        quant(w1m)
+
+        def t_x(q):
+            banks = []
+            for a in range(2):
+                bank = tp_pool.tile([P, 2, 2, P], F32, name="tp", tag="tp")
+                words = xr[q][a][:].bitcast(F32)
+                for t2 in range(2):
+                    for u2 in range(2):
+                        nc.tensor.transpose(bank[:, u2, t2, :], words[:, t2, u2:256:2], ident[:])
+                banks.append(bank)
+            return banks
+
+        def d_x(q, banks, engs):
+            gw = xm[q][0][:].bitcast(F32).rearrange("p (c u) -> p c u", u=2)
+            for a in range(2):
+                copy_on(engs[a], gw[:, 256 * a : 256 * (a + 1), :], banks[a][:].rearrange("p u t m -> p (t m) u"))
+
+        def mul_w(u):
+            nc.vector.tensor_tensor(
+                out=wprod[u][:].rearrange("p i m -> p (i m)"),
+                in0=adj_sb[u][:].rearrange("p i m -> p (i m)"),
+                in1=s_sb[u][:].rearrange("p i m -> p (i m)"),
+                op=MULT,
+            )
+
+        def t_w(u):
+            banks = []
+            words = wprod[u][:].bitcast(F32)
+            for i in range(2):
+                bank = tp_pool.tile([P, 2, 2, P], F32, name="tp", tag="tp")
+                for g in range(2):
+                    for u2 in range(2):
+                        nc.tensor.transpose(bank[:, g, u2, :], words[:, i, 256 * g + u2 : 256 * (g + 1) : 2], ident[:])
+                banks.append(bank)
+            return banks
+
+        def d_w(u, banks, engs):
+            gw = wm[u][0][:].bitcast(F32).rearrange("p (i g r u) -> p i g r u", i=2, g=2, u=2)
+            for i in range(2):
+                copy_on(engs[i], gw[:, i], banks[i][:].rearrange("p g u r -> p g r u"))
+
+        def m_1(q):
+            banks = []
+            for hc in range(4):
+                bank = mm_pool.tile([P, 4, P], S1_DT, name="s1", tag="mm")
+                for t in range(4):
+                    nc.tensor.matmul_mx(
+                        out=bank[:, t, :],
+                        lhsT=xm[q][1][:, P * t : P * (t + 1)].bitcast(FP8X4),
+                        lhsT_scale=xm[q][2][:, P * t : P * (t + 1)],
+                        rhs=w1m[1][:, P * hc : P * (hc + 1)].bitcast(FP8X4),
+                        rhs_scale=w1m[2][:, P * hc : P * (hc + 1)],
+                        start=True,
+                        stop=True,
+                    )
+                banks.append(bank)
+            return banks
+
+        def d_s(q, banks, hc, eng):
+            gv = sm[q][0][:].rearrange("p (h t) -> p h t", t=4)
+            copy_on(eng, gv[:, P * hc : P * (hc + 1), :], banks[hc][:].rearrange("p t h -> p h t"))
+
+        def m_2(u):
+            banks = {}
+            for b in range(2):
+                for i in range(2):
+                    bank = mm_pool.tile([P, H], F32, name="o", tag="mm")
+                    for g in range(2):
+                        c0 = P * (2 * i + g)
+                        nc.tensor.matmul_mx(
+                            out=bank[:],
+                            lhsT=wm[u][1][:, c0 : c0 + P].bitcast(FP8X4),
+                            lhsT_scale=wm[u][2][:, c0 : c0 + P],
+                            rhs=sm[2 * b + g][1][:].bitcast(FP8X4),
+                            rhs_scale=sm[2 * b + g][2][:],
+                            start=(g == 0),
+                            stop=(g == 1),
+                        )
+                    banks[(b, i)] = bank
+            return banks
+
+        def relu_store(u, banks, engs, fine):
+            for b in range(2):
+                stage = keep.tile([P, 2, H], F32, name="ost%d_%d" % (u, b))
+                for i in range(2):
+                    if engs[2 * b + i] == "S":
+                        nc.scalar.activation(out=stage[:, i, :], in_=banks[(b, i)][:], func=RELU)
+                    else:
+                        nc.vector.tensor_scalar_max(stage[:, i, :], banks[(b, i)][:], 0.0)
+                    if fine:
+                        n0 = 256 * u + P * i
+                        nc.sync.dma_start(out=out[b, n0 : n0 + P, :], in_=stage[:, i, :])
+                if not fine:
+                    nc.sync.dma_start(
+                        out=out[b, 256 * u : 256 * (u + 1), :].rearrange("(i p) h -> p i h", p=P), in_=stage[:]
+                    )
+
+        bx = t_x(0)
+        d_x(0, bx, "SV")
+        bx = t_x(1)
+        quant(xm[0])
+        d_x(1, bx, "SV")
+        quant(xm[1])
+        for q in range(4):
+            bs = m_1(q)
+            if q < 2:
+                bn = t_x(q + 2)
+            else:
+                bn = t_w(q - 2)
+            d_s(q, bs, 0, "V")
+            d_s(q, bs, 1, "S")
+            d_s(q, bs, 2, "S")
+            d_s(q, bs, 3, "S")
+            if q >= 1:
+                mul_w(q - 1)
+            if q < 2:
+                d_x(q + 2, bn, "SS")
+            else:
+                d_w(q - 2, bn, "SS")
+            quant(sm[q])
+            if q < 2:
+                quant(xm[q + 2])
+            else:
+                quant(wm[q - 2])
+        for u in range(4):
+            bo = m_2(u)
+            if u < 2:
+                bn = t_w(u + 2)
+            relu_store(u, bo, "SVSV", u == 3)
+            if u == 0:
+                mul_w(3)
+            if u < 2:
+                d_w(u + 2, bn, "SS")
+                quant(wm[u + 2])

@@ -22,8 +22,8 @@ def tile_gcn_pa_kernel(tc, x, adj, S, W1, out):
     nc = tc.nc
     with ExitStack() as ctx:
         keep = ctx.enter_context(tc.tile_pool(name="keep", bufs=1))
-        tp_pool = ctx.enter_context(tc.psum_pool(name="tp", bufs=3))
-        mm_pool = ctx.enter_context(tc.psum_pool(name="mm", bufs=5))
+        tp_pool = ctx.enter_context(tc.psum_pool(name="tp", bufs=4))
+        mm_pool = ctx.enter_context(tc.psum_pool(name="mm", bufs=4))
         ctx.enter_context(tc.manual_schedule())
 
         ident = keep.tile([P, P], F32, name="ident")
@@ -32,7 +32,6 @@ def tile_gcn_pa_kernel(tc, x, adj, S, W1, out):
         warm2 = keep.tile([P, 8], F32, name="warm2")
         nc.vector.memset(warm[:], 0.0)
         nc.scalar.activation(out=warm2[:], in_=warm[:], func=RELU)
-
         zeros = keep.tile([P, 512], BF16, name="zeros")
         nc.vector.memset(zeros[:], 0.0)
         heat = mm_pool.tile([P, 512], F32, name="heat", tag="mm")
@@ -40,9 +39,11 @@ def tile_gcn_pa_kernel(tc, x, adj, S, W1, out):
             nc.tensor.matmul(out=heat[:], lhsT=zeros[:, 0:P], rhs=zeros[:], start=True, stop=True)
 
         w1r = keep.tile([P, 4, H], BF16, name="w1r")
-        nc.sync.dma_start(out=w1r[:], in_=W1.rearrange("(p j) c -> p j c", j=4))
         xf = x.rearrange("b m f -> (b m) f")
-        xr, adj_sb, s_sb = [], [], []
+        xr, adj_sb, s_sb = {}, {}, {}
+
+        def load_w1():
+            nc.sync.dma_start(out=w1r[:], in_=W1.rearrange("(p j) c -> p j c", j=4))
 
         def load_x(q):
             src = xf[512 * q : 512 * (q + 1), :].rearrange("(m t) f -> m t f", t=4)
@@ -51,16 +52,17 @@ def tile_gcn_pa_kernel(tc, x, adj, S, W1, out):
                 t_ = keep.tile([P, 2, F], BF16, name="xr%d_%d" % (q, a))
                 nc.sync.dma_start(out=t_[:], in_=src[:, 2 * a : 2 * a + 2, :])
                 halves.append(t_)
-            xr.append(halves)
+            xr[q] = halves
 
         def load_w(u):
             a_ = keep.tile([P, 2, N], BF16, name="adj%d" % u)
             nc.sync.dma_start(out=a_[:], in_=adj[256 * u : 256 * (u + 1), :].rearrange("(i p) m -> p i m", p=P))
             s_ = keep.tile([P, 2, N], BF16, name="s%d" % u)
             nc.sync.dma_start(out=s_[:], in_=S[256 * u : 256 * (u + 1), :].rearrange("(i p) m -> p i m", p=P))
-            adj_sb.append(a_)
-            s_sb.append(s_)
+            adj_sb[u] = a_
+            s_sb[u] = s_
 
+        load_w1()
         load_x(0)
         load_x(1)
         load_x(2)
@@ -91,12 +93,14 @@ def tile_gcn_pa_kernel(tc, x, adj, S, W1, out):
         sm = [mx_tiles("sp%d" % q) for q in range(4)]
         wm = [mx_tiles("w%d" % u) for u in range(4)]
         wprod = [keep.tile([P, 2, N], BF16, name="wprod%d" % u) for u in range(4)]
+        bx, bw, bs, bo = {}, {}, {}, {}
 
-        nc.vector.tensor_copy(
-            out=w1m[0][:].rearrange("p (c j) -> p c j", j=4),
-            in_=w1r[:].rearrange("p j c -> p c j"),
-        )
-        quant(w1m)
+        def prep_w1():
+            nc.vector.tensor_copy(
+                out=w1m[0][:].rearrange("p (c j) -> p c j", j=4),
+                in_=w1r[:].rearrange("p j c -> p c j"),
+            )
+            quant(w1m)
 
         def t_x(q):
             banks = []
@@ -107,12 +111,12 @@ def tile_gcn_pa_kernel(tc, x, adj, S, W1, out):
                     for u2 in range(2):
                         nc.tensor.transpose(bank[:, u2, t2, :], words[:, t2, u2:256:2], ident[:])
                 banks.append(bank)
-            return banks
+            bx[q] = banks
 
-        def d_x(q, banks, engs):
+        def d_x(q, engs):
             gw = xm[q][0][:].bitcast(F32).rearrange("p (c u) -> p c u", u=2)
             for a in range(2):
-                copy_on(engs[a], gw[:, 256 * a : 256 * (a + 1), :], banks[a][:].rearrange("p u t m -> p (t m) u"))
+                copy_on(engs[a], gw[:, 256 * a : 256 * (a + 1), :], bx[q][a][:].rearrange("p u t m -> p (t m) u"))
 
         def mul_w(u):
             nc.vector.tensor_tensor(
@@ -131,12 +135,12 @@ def tile_gcn_pa_kernel(tc, x, adj, S, W1, out):
                     for u2 in range(2):
                         nc.tensor.transpose(bank[:, g, u2, :], words[:, i, 256 * g + u2 : 256 * (g + 1) : 2], ident[:])
                 banks.append(bank)
-            return banks
+            bw[u] = banks
 
-        def d_w(u, banks, engs):
+        def d_w(u, engs):
             gw = wm[u][0][:].bitcast(F32).rearrange("p (i g r u) -> p i g r u", i=2, g=2, u=2)
             for i in range(2):
-                copy_on(engs[i], gw[:, i], banks[i][:].rearrange("p g u r -> p g r u"))
+                copy_on(engs[i], gw[:, i], bw[u][i][:].rearrange("p g u r -> p g r u"))
 
         def m_1(q):
             banks = []
@@ -153,81 +157,98 @@ def tile_gcn_pa_kernel(tc, x, adj, S, W1, out):
                         stop=True,
                     )
                 banks.append(bank)
-            return banks
+            bs[q] = banks
 
-        def d_s(q, banks, hc, eng):
+        def d_s(q, engs):
             gv = sm[q][0][:].rearrange("p (h t) -> p h t", t=4)
-            copy_on(eng, gv[:, P * hc : P * (hc + 1), :], banks[hc][:].rearrange("p t h -> p h t"))
+            for hc in range(4):
+                copy_on(engs[hc], gv[:, P * hc : P * (hc + 1), :], bs[q][hc][:].rearrange("p t h -> p h t"))
 
-        def m_2(u):
-            banks = {}
-            for b in range(2):
-                for i in range(2):
-                    bank = mm_pool.tile([P, H], F32, name="o", tag="mm")
-                    for g in range(2):
-                        c0 = P * (2 * i + g)
-                        nc.tensor.matmul_mx(
-                            out=bank[:],
-                            lhsT=wm[u][1][:, c0 : c0 + P].bitcast(FP8X4),
-                            lhsT_scale=wm[u][2][:, c0 : c0 + P],
-                            rhs=sm[2 * b + g][1][:].bitcast(FP8X4),
-                            rhs_scale=sm[2 * b + g][2][:],
-                            start=(g == 0),
-                            stop=(g == 1),
-                        )
-                    banks[(b, i)] = bank
-            return banks
-
-        def relu_store(u, banks, engs, fine):
-            for b in range(2):
-                stage = keep.tile([P, 2, H], F32, name="ost%d_%d" % (u, b))
-                for i in range(2):
-                    if engs[2 * b + i] == "S":
-                        nc.scalar.activation(out=stage[:, i, :], in_=banks[(b, i)][:], func=RELU)
-                    else:
-                        nc.vector.tensor_scalar_max(stage[:, i, :], banks[(b, i)][:], 0.0)
-                    if fine:
-                        n0 = 256 * u + P * i
-                        nc.sync.dma_start(out=out[b, n0 : n0 + P, :], in_=stage[:, i, :])
-                if not fine:
-                    nc.sync.dma_start(
-                        out=out[b, 256 * u : 256 * (u + 1), :].rearrange("(i p) h -> p i h", p=P), in_=stage[:]
+        def m_2(b, u):
+            banks = []
+            for i in range(2):
+                bank = mm_pool.tile([P, H], F32, name="o", tag="mm")
+                for g in range(2):
+                    c0 = P * (2 * i + g)
+                    nc.tensor.matmul_mx(
+                        out=bank[:],
+                        lhsT=wm[u][1][:, c0 : c0 + P].bitcast(FP8X4),
+                        lhsT_scale=wm[u][2][:, c0 : c0 + P],
+                        rhs=sm[2 * b + g][1][:].bitcast(FP8X4),
+                        rhs_scale=sm[2 * b + g][2][:],
+                        start=(g == 0),
+                        stop=(g == 1),
                     )
+                banks.append(bank)
+            bo[(b, u)] = banks
 
-        bx = t_x(0)
-        d_x(0, bx, "SV")
-        bx = t_x(1)
+        def relu_store(b, u, engs, fine):
+            stage = keep.tile([P, 2, H], F32, name="ost%d_%d" % (u, b))
+            for i in range(2):
+                if engs[i] == "S":
+                    nc.scalar.activation(out=stage[:, i, :], in_=bo[(b, u)][i][:], func=RELU)
+                else:
+                    nc.vector.tensor_scalar_max(stage[:, i, :], bo[(b, u)][i][:], 0.0)
+                if fine:
+                    n0 = 256 * u + P * i
+                    nc.sync.dma_start(out=out[b, n0 : n0 + P, :], in_=stage[:, i, :])
+            if not fine:
+                nc.sync.dma_start(out=out[b, 256 * u : 256 * (u + 1), :].rearrange("(i p) h -> p i h", p=P), in_=stage[:])
+
+        t_x(0)
+        t_x(1)
+        d_x(0, "SS")
+        prep_w1()
         quant(xm[0])
-        d_x(1, bx, "SV")
+        d_x(1, "SV")
         quant(xm[1])
-        for q in range(4):
-            bs = m_1(q)
-            if q < 2:
-                bn = t_x(q + 2)
-            else:
-                bn = t_w(q - 2)
-            d_s(q, bs, 0, "V")
-            d_s(q, bs, 1, "S")
-            d_s(q, bs, 2, "S")
-            d_s(q, bs, 3, "S")
-            if q >= 1:
-                mul_w(q - 1)
-            if q < 2:
-                d_x(q + 2, bn, "SS")
-            else:
-                d_w(q - 2, bn, "SS")
-            quant(sm[q])
-            if q < 2:
-                quant(xm[q + 2])
-            else:
-                quant(wm[q - 2])
-        for u in range(4):
-            bo = m_2(u)
-            if u < 2:
-                bn = t_w(u + 2)
-            relu_store(u, bo, "SVSV", u == 3)
-            if u == 0:
-                mul_w(3)
-            if u < 2:
-                d_w(u + 2, bn, "SS")
-                quant(wm[u + 2])
+        m_1(0)
+        t_x(2)
+        d_s(0, "SVSS")
+        d_x(2, "VS")
+        quant(sm[0])
+        m_1(1)
+        t_x(3)
+        d_s(1, "VSSS")
+        quant(xm[2])
+        mul_w(0)
+        d_x(3, "SS")
+        m_1(2)
+        t_w(0)
+        d_s(2, "VSSS")
+        quant(sm[1])
+        quant(xm[3])
+        mul_w(1)
+        quant(sm[2])
+        d_w(0, "SS")
+        quant(wm[0])
+        m_1(3)
+        t_w(1)
+        mul_w(2)
+        d_s(3, "SSSS")
+        quant(sm[3])
+        d_w(1, "SV")
+        quant(wm[1])
+        m_2(0, 0)
+        t_w(2)
+        m_2(1, 0)
+        relu_store(0, 0, "SS", False)
+        relu_store(1, 0, "SV", False)
+        mul_w(3)
+        d_w(2, "VS")
+        m_2(0, 1)
+        m_2(1, 1)
+        t_w(3)
+        relu_store(0, 1, "SS", False)
+        quant(wm[2])
+        relu_store(1, 1, "SS", False)
+        d_w(3, "SV")
+        m_2(0, 2)
+        relu_store(0, 2, "VS", True)
+        quant(wm[3])
+        m_2(1, 2)
+        relu_store(1, 2, "SV", True)
+        m_2(0, 3)
+        relu_store(0, 3, "VS", True)
+        m_2(1, 3)
+        relu_store(1, 3, "VV", True)

@@ -120,9 +120,9 @@ def tile_gcn_pa_kernel(tc, x, adj, S, W1, out):
 
         def mul_w(u):
             nc.vector.tensor_tensor(
-                out=wprod[u][:].rearrange("p i m -> p (i m)"),
-                in0=adj_sb[u][:].rearrange("p i m -> p (i m)"),
-                in1=s_sb[u][:].rearrange("p i m -> p (i m)"),
+                out=wprod[u][:].rearrange("p v (k e) -> p k v e", e=2),
+                in0=adj_sb[u][:].rearrange("p i (k v e) -> p (i k) v e", v=2, e=2),
+                in1=s_sb[u][:].rearrange("p i (k v e) -> p (i k) v e", v=2, e=2),
                 op=MULT,
             )
 
@@ -133,7 +133,7 @@ def tile_gcn_pa_kernel(tc, x, adj, S, W1, out):
                 bank = tp_pool.tile([P, 2, 2, P], F32, name="tp", tag="tp")
                 for g in range(2):
                     for u2 in range(2):
-                        nc.tensor.transpose(bank[:, g, u2, :], words[:, i, 256 * g + u2 : 256 * (g + 1) : 2], ident[:])
+                        nc.tensor.transpose(bank[:, g, u2, :], words[:, u2, P * (2 * i + g) : P * (2 * i + g + 1)], ident[:])
                 banks.append(bank)
             bw[u] = banks
 

@@ -200,7 +200,7 @@ def tile_gcn_pa_kernel(tc, x, adj, S, W1, out):
         d_x(0, "SS")
         prep_w1()
         quant(xm[0])
-        d_x(1, "SV")
+        d_x(1, "SS")
         quant(xm[1])
         m_1(0)
         t_x(2)
@@ -233,7 +233,7 @@ def tile_gcn_pa_kernel(tc, x, adj, S, W1, out):
         t_w(2)
         m_2(1, 0)
         relu_store(0, 0, "SS", False)
-        relu_store(1, 0, "SV", False)
+        relu_store(1, 0, "SS", False)
         mul_w(3)
         d_w(2, "VS")
         m_2(0, 1)
@@ -251,4 +251,4 @@ def tile_gcn_pa_kernel(tc, x, adj, S, W1, out):
         m_2(0, 3)
         relu_store(0, 3, "VS", True)
         m_2(1, 3)
-        relu_store(1, 3, "VV", True)
+        relu_store(1, 3, "SV", True)

@@ -15,7 +15,7 @@ B, N, F, H = 2, 1024, 512, 512
 FLOPS = 2 * B * N * F * H + 2 * B * N * N * H
 P = 128
 S1_DT = BF16
-N_HEAT = 6
+N_HEAT = 4
 
 
 def tile_gcn_pa_kernel(tc, x, adj, S, W1, out):
@@ -45,6 +45,15 @@ def tile_gcn_pa_kernel(tc, x, adj, S, W1, out):
         def load_w1():
             nc.sync.dma_start(out=w1r[:], in_=W1.rearrange("(p j) c -> p j c", j=4))
 
+        x0s = []
+
+        def load_x0():
+            src = xf[0:512, :].rearrange("(m t) f -> m t f", t=4)
+            for t in range(4):
+                t_ = keep.tile([P, F], BF16, name="x0s%d" % t)
+                nc.sync.dma_start(out=t_[:], in_=src[:, t, :])
+                x0s.append(t_)
+
         def load_x(q):
             src = xf[512 * q : 512 * (q + 1), :].rearrange("(m t) f -> m t f", t=4)
             halves = []
@@ -63,7 +72,7 @@ def tile_gcn_pa_kernel(tc, x, adj, S, W1, out):
             s_sb[u] = s_
 
         load_w1()
-        load_x(0)
+        load_x0()
         load_x(1)
         load_x(2)
         load_w(0)
@@ -82,6 +91,12 @@ def tile_gcn_pa_kernel(tc, x, adj, S, W1, out):
             g, c, s = t3
             nc.vector.quantize_mx(out=c[:].bitcast(FP8X4), scales=s[:], in_=g[:])
 
+        def quant_half(t3, a):
+            g, c, s = t3
+            nc.vector.quantize_mx(
+                out=c[:, 256 * a : 256 * (a + 1)].bitcast(FP8X4), scales=s[:, 256 * a : 256 * (a + 1)], in_=g[:, 1024 * a : 1024 * (a + 1)]
+            )
+
         def copy_on(eng, out_, in_):
             if eng == "S":
                 nc.scalar.copy(out=out_, in_=in_)
@@ -95,12 +110,31 @@ def tile_gcn_pa_kernel(tc, x, adj, S, W1, out):
         wprod = [keep.tile([P, 2, N], BF16, name="wprod%d" % u) for u in range(4)]
         bx, bw, bs, bo = {}, {}, {}, {}
 
+        W1_CUT = 368
+
         def prep_w1():
-            nc.vector.tensor_copy(
-                out=w1m[0][:].rearrange("p (c j) -> p c j", j=4),
-                in_=w1r[:].rearrange("p j c -> p c j"),
-            )
+            o_ = w1m[0][:].rearrange("p (c j) -> p c j", j=4)
+            i_ = w1r[:].rearrange("p j c -> p c j")
+            nc.scalar.copy(out=o_[:, W1_CUT:H, :], in_=i_[:, W1_CUT:H, :])
+            nc.vector.tensor_copy(out=o_[:, 0:W1_CUT, :], in_=i_[:, 0:W1_CUT, :])
             quant(w1m)
+
+        b0 = []
+
+        def t_x0(t):
+            bank = tp_pool.tile([P, 2, P], F32, name="tp", tag="tp")
+            words = x0s[t][:].bitcast(F32)
+            for u2 in range(2):
+                nc.tensor.transpose(bank[:, u2, :], words[:, u2:256:2], ident[:])
+            b0.append(bank)
+
+        def d_x0(t, eng):
+            gw = xm[0][0][:].bitcast(F32).rearrange("p (c u) -> p c u", u=2)
+            copy_on(eng, gw[:, P * t : P * (t + 1), :], b0[t][:].rearrange("p u m -> p m u"))
+
+        def quant_part(t3, c0, c1):
+            g, c, s = t3
+            nc.vector.quantize_mx(out=c[:, c0:c1].bitcast(FP8X4), scales=s[:, c0:c1], in_=g[:, 4 * c0 : 4 * c1])
 
         def t_x(q):
             banks = []
@@ -195,13 +229,18 @@ def tile_gcn_pa_kernel(tc, x, adj, S, W1, out):
             if not fine:
                 nc.sync.dma_start(out=out[b, 256 * u : 256 * (u + 1), :].rearrange("(i p) h -> p i h", p=P), in_=stage[:])
 
-        t_x(0)
+        for t in range(4):
+            t_x0(t)
         t_x(1)
-        d_x(0, "SS")
         prep_w1()
-        quant(xm[0])
+        for t in range(4):
+            d_x0(t, "S")
+        quant_part(xm[0], 0, 256)
+        quant_part(xm[0], 256, 384)
+        quant_part(xm[0], 384, 512)
         d_x(1, "SS")
-        quant(xm[1])
+        quant_half(xm[1], 0)
+        quant_half(xm[1], 1)
         m_1(0)
         t_x(2)
         d_s(0, "SVSS")

@@ -65,9 +65,9 @@ def tile_gcn_pa_kernel(tc, x, adj, S, W1, out):
 
         def load_w(u):
             a_ = keep.tile([P, 2, N], BF16, name="adj%d" % u)
-            nc.sync.dma_start(out=a_[:], in_=adj[256 * u : 256 * (u + 1), :].rearrange("(i p) m -> p i m", p=P))
+            nc.sync.dma_start(out=a_[:], in_=adj[256 * u : 256 * (u + 1), :].rearrange("(p i) m -> p i m", i=2))
             s_ = keep.tile([P, 2, N], BF16, name="s%d" % u)
-            nc.sync.dma_start(out=s_[:], in_=S[256 * u : 256 * (u + 1), :].rearrange("(i p) m -> p i m", p=P))
+            nc.sync.dma_start(out=s_[:], in_=S[256 * u : 256 * (u + 1), :].rearrange("(p i) m -> p i m", i=2))
             adj_sb[u] = a_
             s_sb[u] = s_
 
@@ -224,10 +224,9 @@ def tile_gcn_pa_kernel(tc, x, adj, S, W1, out):
                 else:
                     nc.vector.tensor_scalar_max(stage[:, i, :], bo[(b, u)][i][:], 0.0)
                 if fine:
-                    n0 = 256 * u + P * i
-                    nc.sync.dma_start(out=out[b, n0 : n0 + P, :], in_=stage[:, i, :])
+                    nc.sync.dma_start(out=out[b, 256 * u + i : 256 * (u + 1) : 2, :], in_=stage[:, i, :])
             if not fine:
-                nc.sync.dma_start(out=out[b, 256 * u : 256 * (u + 1), :].rearrange("(i p) h -> p i h", p=P), in_=stage[:])
+                nc.sync.dma_start(out=out[b, 256 * u : 256 * (u + 1), :].rearrange("(p i) h -> p i h", i=2), in_=stage[:])
 
         for t in range(4):
             t_x0(t)

from contextlib import ExitStack

import concourse.mybir as mybir
from concourse.masks import make_identity

F32 = mybir.dt.float32
BF16 = mybir.dt.bfloat16
U32 = mybir.dt.uint32
U8 = mybir.dt.uint8
FP8X4 = mybir.dt.float8_e4m3fn_x4
RELU = mybir.ActivationFunctionType.Relu
MULT = mybir.AluOpType.mult

B, N, F, H = 2, 1024, 512, 512
FLOPS = 2 * B * N * F * H + 2 * B * N * N * H
P = 128
S1_DT = BF16
N_HEAT = 4


def tile_gcn_pa_kernel(tc, x, adj, S, W1, out):
    nc = tc.nc
    with ExitStack() as ctx:
        keep = ctx.enter_context(tc.tile_pool(name="keep", bufs=1))
        tp_pool = ctx.enter_context(tc.psum_pool(name="tp", bufs=4))
        mm_pool = ctx.enter_context(tc.psum_pool(name="mm", bufs=4))
        ctx.enter_context(tc.manual_schedule())

        ident = keep.tile([P, P], F32, name="ident")
        make_identity(nc, ident[:])
        warm = keep.tile([P, 8], F32, name="warm")
        warm2 = keep.tile([P, 8], F32, name="warm2")
        nc.vector.memset(warm[:], 0.0)
        nc.scalar.activation(out=warm2[:], in_=warm[:], func=RELU)
        zeros = keep.tile([P, 512], BF16, name="zeros")
        nc.vector.memset(zeros[:], 0.0)
        heat = mm_pool.tile([P, 512], F32, name="heat", tag="mm")
        for k in range(N_HEAT):
            nc.tensor.matmul(out=heat[:], lhsT=zeros[:, 0:P], rhs=zeros[:], start=True, stop=True)

        w1r = keep.tile([P, 4, H], BF16, name="w1r")
        xf = x.rearrange("b m f -> (b m) f")
        xr, adj_sb, s_sb = {}, {}, {}

        def load_w1():
            nc.sync.dma_start(out=w1r[:], in_=W1.rearrange("(p j) c -> p j c", j=4))

        x0s = []

        def load_x0():
            src = xf[0:512, :].rearrange("(m t) f -> m t f", t=4)
            for t in range(4):
                t_ = keep.tile([P, F], BF16, name="x0s%d" % t)
                nc.sync.dma_start(out=t_[:], in_=src[:, t, :])
                x0s.append(t_)

        def load_x(q):
            src = xf[512 * q : 512 * (q + 1), :].rearrange("(m t) f -> m t f", t=4)
            halves = []
            for a in range(2):
                t_ = keep.tile([P, 2, F], BF16, name="xr%d_%d" % (q, a))
                nc.sync.dma_start(out=t_[:], in_=src[:, 2 * a : 2 * a + 2, :])
                halves.append(t_)
            xr[q] = halves

        def load_w(u):
            a_ = keep.tile([P, 2, N], BF16, name="adj%d" % u)
            nc.sync.dma_start(out=a_[:], in_=adj[256 * u : 256 * (u + 1), :].rearrange("(p i) m -> p i m", i=2))
            s_ = keep.tile([P, 2, N], BF16, name="s%d" % u)
            nc.sync.dma_start(out=s_[:], in_=S[256 * u : 256 * (u + 1), :].rearrange("(p i) m -> p i m", i=2))
            adj_sb[u] = a_
            s_sb[u] = s_

        load_w1()
        load_x0()
        load_x(1)
        load_x(2)
        load_w(0)
        load_x(3)
        load_w(1)
        load_w(2)
        load_w(3)

        def mx_tiles(tag):
            g = keep.tile([P, 2048], BF16, name=tag + "g", align_bytes=64)
            c = keep.tile([P, 512], U32, name=tag + "c", align_bytes=64)
            s = keep.tile([P, 512], U8, name=tag + "s", align_bytes=64)
            return g, c, s

        def quant(t3):
            g, c, s = t3
            nc.vector.quantize_mx(out=c[:].bitcast(FP8X4), scales=s[:], in_=g[:])

        def quant_half(t3, a):
            g, c, s = t3
            nc.vector.quantize_mx(
                out=c[:, 256 * a : 256 * (a + 1)].bitcast(FP8X4), scales=s[:, 256 * a : 256 * (a + 1)], in_=g[:, 1024 * a : 1024 * (a + 1)]
            )

        def copy_on(eng, out_, in_):
            if eng == "S":
                nc.scalar.copy(out=out_, in_=in_)
            else:
                nc.vector.tensor_copy(out=out_, in_=in_)

        w1m = mx_tiles("w1")
        xm = [mx_tiles("x%d" % q) for q in range(4)]
        sm = [mx_tiles("sp%d" % q) for q in range(4)]
        wm = [mx_tiles("w%d" % u) for u in range(4)]
        wprod = [keep.tile([P, 2, N], BF16, name="wprod%d" % u) for u in range(4)]
        bx, bw, bs, bo = {}, {}, {}, {}

        W1_CUT = 368

        def prep_w1():
            o_ = w1m[0][:].rearrange("p (c j) -> p c j", j=4)
            i_ = w1r[:].rearrange("p j c -> p c j")
            nc.scalar.copy(out=o_[:, W1_CUT:H, :], in_=i_[:, W1_CUT:H, :])
            nc.vector.tensor_copy(out=o_[:, 0:W1_CUT, :], in_=i_[:, 0:W1_CUT, :])
            quant(w1m)

        b0 = []

        def t_x0(t):
            bank = tp_pool.tile([P, 2, P], F32, name="tp", tag="tp")
            words = x0s[t][:].bitcast(F32)
            for u2 in range(2):
                nc.tensor.transpose(bank[:, u2, :], words[:, u2:256:2], ident[:])
            b0.append(bank)

        def d_x0(t, eng):
            gw = xm[0][0][:].bitcast(F32).rearrange("p (c u) -> p c u", u=2)
            copy_on(eng, gw[:, P * t : P * (t + 1), :], b0[t][:].rearrange("p u m -> p m u"))

        def quant_part(t3, c0, c1):
            g, c, s = t3
            nc.vector.quantize_mx(out=c[:, c0:c1].bitcast(FP8X4), scales=s[:, c0:c1], in_=g[:, 4 * c0 : 4 * c1])

        def t_x(q):
            banks = []
            for a in range(2):
                bank = tp_pool.tile([P, 2, 2, P], F32, name="tp", tag="tp")
                words = xr[q][a][:].bitcast(F32)
                for t2 in range(2):
                    for u2 in range(2):
                        nc.tensor.transpose(bank[:, u2, t2, :], words[:, t2, u2:256:2], ident[:])
                banks.append(bank)
            bx[q] = banks

        def d_x(q, engs):
            gw = xm[q][0][:].bitcast(F32).rearrange("p (c u) -> p c u", u=2)
            for a in range(2):
                copy_on(engs[a], gw[:, 256 * a : 256 * (a + 1), :], bx[q][a][:].rearrange("p u t m -> p (t m) u"))

        def mul_w(u):
            nc.vector.tensor_tensor(
                out=wprod[u][:].rearrange("p v (k e) -> p k v e", e=2),
                in0=adj_sb[u][:].rearrange("p i (k v e) -> p (i k) v e", v=2, e=2),
                in1=s_sb[u][:].rearrange("p i (k v e) -> p (i k) v e", v=2, e=2),
                op=MULT,
            )

        def t_w(u):
            banks = []
            words = wprod[u][:].bitcast(F32)
            for i in range(2):
                bank = tp_pool.tile([P, 2, 2, P], F32, name="tp", tag="tp")
                for g in range(2):
                    for u2 in range(2):
                        nc.tensor.transpose(bank[:, g, u2, :], words[:, u2, P * (2 * i + g) : P * (2 * i + g + 1)], ident[:])
                banks.append(bank)
            bw[u] = banks

        def d_w(u, engs):
            gw = wm[u][0][:].bitcast(F32).rearrange("p (i g r u) -> p i g r u", i=2, g=2, u=2)
            for i in range(2):
                copy_on(engs[i], gw[:, i], bw[u][i][:].rearrange("p g u r -> p g r u"))

        def m_1(q):
            banks = []
            for hc in range(4):
                bank = mm_pool.tile([P, 4, P], S1_DT, name="s1", tag="mm")
                for t in range(4):
                    nc.tensor.matmul_mx(
                        out=bank[:, t, :],
                        lhsT=xm[q][1][:, P * t : P * (t + 1)].bitcast(FP8X4),
                        lhsT_scale=xm[q][2][:, P * t : P * (t + 1)],
                        rhs=w1m[1][:, P * hc : P * (hc + 1)].bitcast(FP8X4),
                        rhs_scale=w1m[2][:, P * hc : P * (hc + 1)],
                        start=True,
                        stop=True,
                    )
                banks.append(bank)
            bs[q] = banks

        def d_s(q, engs):
            gv = sm[q][0][:].rearrange("p (h t) -> p h t", t=4)
            for hc in range(4):
                copy_on(engs[hc], gv[:, P * hc : P * (hc + 1), :], bs[q][hc][:].rearrange("p t h -> p h t"))

        def m_2(b, u):
            banks = []
            for i in range(2):
                bank = mm_pool.tile([P, H], F32, name="o", tag="mm")
                for g in range(2):
                    c0 = P * (2 * i + g)
                    nc.tensor.matmul_mx(
                        out=bank[:],
                        lhsT=wm[u][1][:, c0 : c0 + P].bitcast(FP8X4),
                        lhsT_scale=wm[u][2][:, c0 : c0 + P],
                        rhs=sm[2 * b + g][1][:].bitcast(FP8X4),
                        rhs_scale=sm[2 * b + g][2][:],
                        start=(g == 0),
                        stop=(g == 1),
                    )
                banks.append(bank)
            bo[(b, u)] = banks

        def relu_store(b, u, engs, fine):
            stage = keep.tile([P, 2, H], F32, name="ost%d_%d" % (u, b))
            for i in range(2):
                if engs[i] == "S":
                    nc.scalar.activation(out=stage[:, i, :], in_=bo[(b, u)][i][:], func=RELU)
                else:
                    nc.vector.tensor_scalar_max(stage[:, i, :], bo[(b, u)][i][:], 0.0)
                if fine:
                    nc.sync.dma_start(out=out[b, 256 * u + i : 256 * (u + 1) : 2, :], in_=stage[:, i, :])
            if not fine:
                nc.sync.dma_start(out=out[b, 256 * u : 256 * (u + 1), :].rearrange("(p i) h -> p i h", i=2), in_=stage[:])

        for t in range(4):
            t_x0(t)
        t_x(1)
        prep_w1()
        for t in range(4):
            d_x0(t, "S")
        quant_part(xm[0], 0, 256)
        quant_part(xm[0], 256, 384)
        quant_part(xm[0], 384, 512)
        d_x(1, "SS")
        quant_half(xm[1], 0)
        quant_half(xm[1], 1)
        m_1(0)
        t_x(2)
        d_s(0, "SVSS")
        d_x(2, "VS")
        quant(sm[0])
        m_1(1)
        t_x(3)
        d_s(1, "VSSS")
        quant(xm[2])
        mul_w(0)
        d_x(3, "SS")
        m_1(2)
        t_w(0)
        d_s(2, "VSSS")
        quant(sm[1])
        quant(xm[3])
        mul_w(1)
        quant(sm[2])
        d_w(0, "SS")
        quant(wm[0])
        m_1(3)
        t_w(1)
        mul_w(2)
        d_s(3, "SSSS")
        quant(sm[3])
        d_w(1, "SV")
        quant(wm[1])
        m_2(0, 0)
        t_w(2)
        m_2(1, 0)
        relu_store(0, 0, "SS", False)
        relu_store(1, 0, "SS", False)
        mul_w(3)
        d_w(2, "VS")
        m_2(0, 1)
        m_2(1, 1)
        t_w(3)
        relu_store(0, 1, "SS", False)
        quant(wm[2])
        relu_store(1, 1, "SS", False)
        d_w(3, "SV")
        m_2(0, 2)
        relu_store(0, 2, "VS", True)
        quant(wm[3])
        m_2(1, 2)
        relu_store(1, 2, "SV", True)
        m_2(0, 3)
        relu_store(0, 3, "VS", True)
        m_2(1, 3)
        relu_store(1, 3, "SV", True)
